import numpy as np
import ml_dtypes

BF16 = ml_dtypes.bfloat16


def bf(x):
    return np.asarray(x, np.float32).astype(BF16)


def f32(x):
    return np.asarray(x, np.float32)


def f64(x):
    return np.asarray(x).astype(np.float64)


def striped(idx):
    return np.tile(idx.reshape(-1, 16).T, (8, 1))


B, L, D, C, S, N, AW = 2, 128, 256, 384, 1024, 256, 4


def position_weight(start, end):
    pos = np.arange(L)
    return np.where(pos < start, 1.0 - (start - pos) / L, np.where(pos > end, 1.0 - (pos - end) / L, 0.0))


def setup_inputs():
    starts = np.random.permutation(L - AW)[:B]
    pw = np.concatenate([position_weight(s0, s0 + AW - 1) for s0 in starts])[None, :]
    return {"base": f32(0.5 * np.random.standard_normal((C, S))), "h": f32(np.random.standard_normal((D, N))), "pw": f32(pw), "w": bf(0.5 * np.random.standard_normal((D, C)) / np.sqrt(D)), "b": f32(0.1 * np.random.standard_normal((C, 1))), "offs": striped(np.random.permutation(S)[:N])}


def reference(base, h, pw, w, b, offs):
    idx = offs[:16].T.reshape(-1)
    out = f64(base).copy()
    out[:, idx] = f64(w).T @ (f64(h) * f64(pw)) + f64(b)
    return out

@@ -1,0 +1,64 @@
+import concourse.mybir as mybir
+
+F32, BF16, U16 = mybir.dt.float32, mybir.dt.bfloat16, mybir.dt.uint16
+MULT, ADD = mybir.AluOpType.mult, mybir.AluOpType.add
+
+P = 128
+D = 256
+N = 256
+C = 384
+S = 1024
+D_BLOCKS = D // P
+C_BLOCKS = C // P
+
+FLOPS = 2 * D * C * N
+
+
+def tile_typeenhancedgcndeepseek0_kernel(tc, base, h, pw, w, b, offs, out):
+    nc = tc.nc
+    with (
+        tc.tile_pool(name="held", bufs=1) as held,
+        tc.psum_pool(name="psum", bufs=1) as psum,
+    ):
+        offsets = held.tile([P, N // 16], U16, name="offsets")
+        nc.sync.dma_start(offsets[:], offs)
+
+        tokens = [held.tile([P, N], F32, name=f"tokens{k}") for k in range(D_BLOCKS)]
+        for k in range(D_BLOCKS):
+            nc.sync.dma_start(tokens[k][:], h[k * P : (k + 1) * P, :])
+        windows = [held.tile([P, S], F32, name=f"window{t}") for t in range(C_BLOCKS)]
+        for t in range(C_BLOCKS):
+            nc.sync.dma_start(windows[t][:], base[t * P : (t + 1) * P, :])
+
+        weight_of_token = held.tile([P, N], F32, name="weight_of_token")
+        nc.scalar.dma_start(weight_of_token[:], pw.to_broadcast([P, N]))
+        bias = held.tile([P, C_BLOCKS], F32, name="bias")
+        with nc.allow_non_contiguous_dma(reason="384 single floats, one to a partition and block"):
+            nc.scalar.dma_start(bias[:], b.rearrange("(t p) o -> p (t o)", p=P))
+        projection = [held.tile([P, C], BF16, name=f"projection{k}") for k in range(D_BLOCKS)]
+        for k in range(D_BLOCKS):
+            nc.scalar.dma_start(projection[k][:], w[k * P : (k + 1) * P, :])
+
+        bias_of_token = held.tile([P, C_BLOCKS, N], F32, name="bias_of_token")
+        nc.gpsimd.tensor_copy(bias_of_token[:], bias[:].unsqueeze(2).to_broadcast([P, C_BLOCKS, N]))
+
+        weighted = [held.tile([P, N], BF16, name=f"weighted{k}") for k in range(D_BLOCKS)]
+        for k in range(D_BLOCKS):
+            nc.vector.tensor_tensor(weighted[k][:], tokens[k][:], weight_of_token[:], MULT)
+
+        for t in range(C_BLOCKS):
+            product = psum.tile([P, N], F32, name=f"product{t}")
+            for k in range(D_BLOCKS):
+                nc.tensor.matmul(
+                    product[:],
+                    projection[k][:, t * P : (t + 1) * P],
+                    weighted[k][:],
+                    start=(k == 0),
+                    stop=(k == D_BLOCKS - 1),
+                )
+            projected = held.tile([P, N], F32, name=f"projected{t}")
+            nc.scalar.copy(projected[:], product[:])
+            nc.vector.tensor_tensor(
+                windows[t][:].indirect(offsets[:]), projected[:], bias_of_token[:, t, :], ADD
+            )
+            nc.sync.dma_start(out[t * P : (t + 1) * P, :], windows[t][:])

@@ -30,17 +30,23 @@ def tile_typeenhancedgcndeepseek0_kernel(tc, base, h, pw, w, b, offs, out):
         for t in range(C_BLOCKS):
             nc.sync.dma_start(windows[t][:], base[t * P : (t + 1) * P, :])
 
+        bias_row = held.tile([1, C], F32, name="bias_row")
+        nc.scalar.dma_start(bias_row[:], b.rearrange("c o -> o c"))
         weight_of_token = held.tile([P, N], F32, name="weight_of_token")
         nc.scalar.dma_start(weight_of_token[:], pw.to_broadcast([P, N]))
-        bias = held.tile([P, C_BLOCKS], F32, name="bias")
-        with nc.allow_non_contiguous_dma(reason="384 single floats, one to a partition and block"):
-            nc.scalar.dma_start(bias[:], b.rearrange("(t p) o -> p (t o)", p=P))
         projection = [held.tile([P, C], BF16, name=f"projection{k}") for k in range(D_BLOCKS)]
         for k in range(D_BLOCKS):
             nc.scalar.dma_start(projection[k][:], w[k * P : (k + 1) * P, :])
 
+        one = held.tile([1, 1], F32, name="one")
+        nc.gpsimd.memset(one[:], 1.0)
+        bias_column = psum.tile([P, C_BLOCKS], F32, name="bias_column")
+        for t in range(C_BLOCKS):
+            nc.tensor.matmul(
+                bias_column[:, t : t + 1], bias_row[:, t * P : (t + 1) * P], one[:], start=True, stop=True
+            )
         bias_of_token = held.tile([P, C_BLOCKS, N], F32, name="bias_of_token")
-        nc.gpsimd.tensor_copy(bias_of_token[:], bias[:].unsqueeze(2).to_broadcast([P, C_BLOCKS, N]))
+        nc.scalar.copy(bias_of_token[:], bias_column[:].unsqueeze(2).to_broadcast([P, C_BLOCKS, N]))
 
         weighted = [held.tile([P, N], BF16, name=f"weighted{k}") for k in range(D_BLOCKS)]
         for k in range(D_BLOCKS):

@@ -30,21 +30,14 @@ def tile_typeenhancedgcndeepseek0_kernel(tc, base, h, pw, w, b, offs, out):
         for t in range(C_BLOCKS):
             nc.sync.dma_start(windows[t][:], base[t * P : (t + 1) * P, :])
 
-        bias_row = held.tile([1, C], F32, name="bias_row")
-        nc.scalar.dma_start(bias_row[:], b.rearrange("c o -> o c"))
+        bias_column = held.tile([P, C_BLOCKS], F32, name="bias_column")
+        nc.scalar.dma_start(bias_column[:], b.rearrange("(t p) o -> p (t o)", p=P))
         weight_of_token = held.tile([P, N], F32, name="weight_of_token")
         nc.scalar.dma_start(weight_of_token[:], pw.to_broadcast([P, N]))
         projection = [held.tile([P, C], BF16, name=f"projection{k}") for k in range(D_BLOCKS)]
         for k in range(D_BLOCKS):
             nc.scalar.dma_start(projection[k][:], w[k * P : (k + 1) * P, :])
 
-        one = held.tile([1, 1], F32, name="one")
-        nc.gpsimd.memset(one[:], 1.0)
-        bias_column = psum.tile([P, C_BLOCKS], F32, name="bias_column")
-        for t in range(C_BLOCKS):
-            nc.tensor.matmul(
-                bias_column[:, t : t + 1], bias_row[:, t * P : (t + 1) * P], one[:], start=True, stop=True
-            )
         bias_of_token = held.tile([P, C_BLOCKS, N], F32, name="bias_of_token")
         nc.scalar.copy(bias_of_token[:], bias_column[:].unsqueeze(2).to_broadcast([P, C_BLOCKS, N]))
 

@@ -16,22 +16,23 @@ FLOPS = 2 * D * C * N
 
 def tile_typeenhancedgcndeepseek0_kernel(tc, base, h, pw, w, b, offs, out):
     nc = tc.nc
+    base_blocks = base.rearrange("(p t) s -> t p s", t=C_BLOCKS)
+    out_blocks = out.rearrange("(p t) s -> t p s", t=C_BLOCKS)
     with (
         tc.tile_pool(name="held", bufs=1) as held,
         tc.psum_pool(name="psum", bufs=1) as psum,
     ):
-        offsets = held.tile([P, N // 16], U16, name="offsets")
-        nc.sync.dma_start(offsets[:], offs)
-
         tokens = [held.tile([P, N], F32, name=f"tokens{k}") for k in range(D_BLOCKS)]
         for k in range(D_BLOCKS):
             nc.sync.dma_start(tokens[k][:], h[k * P : (k + 1) * P, :])
+        offsets = held.tile([P, N // 16], U16, name="offsets")
+        nc.sync.dma_start(offsets[:], offs)
+        bias_column = held.tile([P, C_BLOCKS], F32, name="bias_column")
+        nc.sync.dma_start(bias_column[:], b.rearrange("(p t) o -> p (t o)", t=C_BLOCKS))
         windows = [held.tile([P, S], F32, name=f"window{t}") for t in range(C_BLOCKS)]
         for t in range(C_BLOCKS):
-            nc.sync.dma_start(windows[t][:], base[t * P : (t + 1) * P, :])
+            nc.sync.dma_start(windows[t][:], base_blocks[t])
 
-        bias_column = held.tile([P, C_BLOCKS], F32, name="bias_column")
-        nc.scalar.dma_start(bias_column[:], b.rearrange("(t p) o -> p (t o)", p=P))
         weight_of_token = held.tile([P, N], F32, name="weight_of_token")
         nc.scalar.dma_start(weight_of_token[:], pw.to_broadcast([P, N]))
         projection = [held.tile([P, C], BF16, name=f"projection{k}") for k in range(D_BLOCKS)]
@@ -50,7 +51,7 @@ def tile_typeenhancedgcndeepseek0_kernel(tc, base, h, pw, w, b, offs, out):
             for k in range(D_BLOCKS):
                 nc.tensor.matmul(
                     product[:],
-                    projection[k][:, t * P : (t + 1) * P],
+                    projection[k][:].rearrange("d (p t) -> d t p", t=C_BLOCKS)[:, t, :],
                     weighted[k][:],
                     start=(k == 0),
                     stop=(k == D_BLOCKS - 1),
@@ -60,4 +61,4 @@ def tile_typeenhancedgcndeepseek0_kernel(tc, base, h, pw, w, b, offs, out):
             nc.vector.tensor_tensor(
                 windows[t][:].indirect(offsets[:]), projected[:], bias_of_token[:, t, :], ADD
             )
-            nc.sync.dma_start(out[t * P : (t + 1) * P, :], windows[t][:])
+            nc.sync.dma_start(out_blocks[t], windows[t][:])

@@ -47,7 +47,7 @@ def tile_typeenhancedgcndeepseek0_kernel(tc, base, h, pw, w, b, offs, out):
             nc.vector.tensor_tensor(weighted[k][:], tokens[k][:], weight_of_token[:], MULT)
 
         for t in range(C_BLOCKS):
-            product = psum.tile([P, N], F32, name=f"product{t}")
+            product = psum.tile([P, N], F32, name="product")
             for k in range(D_BLOCKS):
                 nc.tensor.matmul(
                     product[:],

@@ -39,12 +39,12 @@ def tile_typeenhancedgcndeepseek0_kernel(tc, base, h, pw, w, b, offs, out):
         for k in range(D_BLOCKS):
             nc.scalar.dma_start(projection[k][:], w[k * P : (k + 1) * P, :])
 
-        bias_of_token = held.tile([P, C_BLOCKS, N], F32, name="bias_of_token")
-        nc.scalar.copy(bias_of_token[:], bias_column[:].unsqueeze(2).to_broadcast([P, C_BLOCKS, N]))
-
         weighted = [held.tile([P, N], BF16, name=f"weighted{k}") for k in range(D_BLOCKS)]
         for k in range(D_BLOCKS):
             nc.vector.tensor_tensor(weighted[k][:], tokens[k][:], weight_of_token[:], MULT)
+
+        bias_of_token = held.tile([P, C_BLOCKS, N], F32, name="bias_of_token")
+        nc.vector.tensor_copy(bias_of_token[:], bias_column[:].unsqueeze(2).to_broadcast([P, C_BLOCKS, N]))
 
         for t in range(C_BLOCKS):
             product = psum.tile([P, N], F32, name="product")

@@ -25,10 +25,10 @@ def tile_typeenhancedgcndeepseek0_kernel(tc, base, h, pw, w, b, offs, out):
         tokens = [held.tile([P, N], F32, name=f"tokens{k}") for k in range(D_BLOCKS)]
         for k in range(D_BLOCKS):
             nc.sync.dma_start(tokens[k][:], h[k * P : (k + 1) * P, :])
-        offsets = held.tile([P, N // 16], U16, name="offsets")
-        nc.sync.dma_start(offsets[:], offs)
         bias_column = held.tile([P, C_BLOCKS], F32, name="bias_column")
         nc.sync.dma_start(bias_column[:], b.rearrange("(p t) o -> p (t o)", t=C_BLOCKS))
+        offsets = held.tile([P, N // 16], U16, name="offsets")
+        nc.sync.dma_start(offsets[:], offs)
         windows = [held.tile([P, S], F32, name=f"window{t}") for t in range(C_BLOCKS)]
         for t in range(C_BLOCKS):
             nc.sync.dma_start(windows[t][:], base_blocks[t])
@@ -57,7 +57,10 @@ def tile_typeenhancedgcndeepseek0_kernel(tc, base, h, pw, w, b, offs, out):
                     stop=(k == D_BLOCKS - 1),
                 )
             projected = held.tile([P, N], F32, name=f"projected{t}")
-            nc.scalar.copy(projected[:], product[:])
+            if t == 0:
+                nc.vector.tensor_copy(projected[:], product[:])
+            else:
+                nc.scalar.copy(projected[:], product[:])
             nc.vector.tensor_tensor(
                 windows[t][:].indirect(offsets[:]), projected[:], bias_of_token[:, t, :], ADD
             )

@@ -16,52 +16,56 @@ FLOPS = 2 * D * C * N
 
 def tile_typeenhancedgcndeepseek0_kernel(tc, base, h, pw, w, b, offs, out):
     nc = tc.nc
-    base_blocks = base.rearrange("(p t) s -> t p s", t=C_BLOCKS)
-    out_blocks = out.rearrange("(p t) s -> t p s", t=C_BLOCKS)
     with (
         tc.tile_pool(name="held", bufs=1) as held,
         tc.psum_pool(name="psum", bufs=1) as psum,
     ):
         tokens = [held.tile([P, N], F32, name=f"tokens{k}") for k in range(D_BLOCKS)]
+        weight_of_token = held.tile([P, N], F32, name="weight_of_token")
+        offsets = held.tile([P, N // 16], U16, name="offsets")
+        projection = [held.tile([P, D_BLOCKS, P], BF16, name=f"projection{t}") for t in range(C_BLOCKS)]
+        bias_column = [held.tile([P, 1], F32, name=f"bias_column{t}") for t in range(C_BLOCKS)]
+        windows = [held.tile([P, S], F32, name=f"window{t}") for t in range(C_BLOCKS)]
+
+        def load_projection(queue, t):
+            queue.dma_start(
+                projection[t][:], w[:, t * P : (t + 1) * P].rearrange("(k d) c -> d k c", d=P)
+            )
+
+        nc.scalar.dma_start(weight_of_token[:], pw.to_broadcast([P, N]))
+        load_projection(nc.scalar, 0)
+
         for k in range(D_BLOCKS):
             nc.sync.dma_start(tokens[k][:], h[k * P : (k + 1) * P, :])
-        bias_column = held.tile([P, C_BLOCKS], F32, name="bias_column")
-        nc.sync.dma_start(bias_column[:], b.rearrange("(p t) o -> p (t o)", t=C_BLOCKS))
-        offsets = held.tile([P, N // 16], U16, name="offsets")
-        nc.sync.dma_start(offsets[:], offs)
-        windows = [held.tile([P, S], F32, name=f"window{t}") for t in range(C_BLOCKS)]
         for t in range(C_BLOCKS):
-            nc.sync.dma_start(windows[t][:], base_blocks[t])
-
-        weight_of_token = held.tile([P, N], F32, name="weight_of_token")
-        nc.scalar.dma_start(weight_of_token[:], pw.to_broadcast([P, N]))
-        projection = [held.tile([P, C], BF16, name=f"projection{k}") for k in range(D_BLOCKS)]
-        for k in range(D_BLOCKS):
-            nc.scalar.dma_start(projection[k][:], w[k * P : (k + 1) * P, :])
+            if t > 0:
+                load_projection(nc.sync, t)
+            nc.sync.dma_start(bias_column[t][:], b[t * P : (t + 1) * P, :])
+            if t == 0:
+                nc.sync.dma_start(offsets[:], offs)
+            nc.sync.dma_start(windows[t][:], base[t * P : (t + 1) * P, :])
 
         weighted = [held.tile([P, N], BF16, name=f"weighted{k}") for k in range(D_BLOCKS)]
         for k in range(D_BLOCKS):
             nc.vector.tensor_tensor(weighted[k][:], tokens[k][:], weight_of_token[:], MULT)
-
-        bias_of_token = held.tile([P, C_BLOCKS, N], F32, name="bias_of_token")
-        nc.vector.tensor_copy(bias_of_token[:], bias_column[:].unsqueeze(2).to_broadcast([P, C_BLOCKS, N]))
 
         for t in range(C_BLOCKS):
             product = psum.tile([P, N], F32, name="product")
             for k in range(D_BLOCKS):
                 nc.tensor.matmul(
                     product[:],
-                    projection[k][:].rearrange("d (p t) -> d t p", t=C_BLOCKS)[:, t, :],
+                    projection[t][:, k, :],
                     weighted[k][:],
                     start=(k == 0),
                     stop=(k == D_BLOCKS - 1),
                 )
+            bias_of_token = held.tile([P, N], F32, name=f"bias_of_token{t}")
             projected = held.tile([P, N], F32, name=f"projected{t}")
             if t == 0:
+                nc.vector.tensor_copy(bias_of_token[:], bias_column[t][:].to_broadcast([P, N]))
                 nc.vector.tensor_copy(projected[:], product[:])
             else:
+                nc.scalar.copy(bias_of_token[:], bias_column[t][:].to_broadcast([P, N]))
                 nc.scalar.copy(projected[:], product[:])
-            nc.vector.tensor_tensor(
-                windows[t][:].indirect(offsets[:]), projected[:], bias_of_token[:, t, :], ADD
-            )
-            nc.sync.dma_start(out_blocks[t], windows[t][:])
+            nc.vector.tensor_tensor(windows[t][:].indirect(offsets[:]), projected[:], bias_of_token[:], ADD)
+            nc.sync.dma_start(out[t * P : (t + 1) * P, :], windows[t][:])

@@ -38,11 +38,11 @@ def tile_typeenhancedgcndeepseek0_kernel(tc, base, h, pw, w, b, offs, out):
         for k in range(D_BLOCKS):
             nc.sync.dma_start(tokens[k][:], h[k * P : (k + 1) * P, :])
         for t in range(C_BLOCKS):
-            if t > 0:
-                load_projection(nc.sync, t)
             nc.sync.dma_start(bias_column[t][:], b[t * P : (t + 1) * P, :])
             if t == 0:
                 nc.sync.dma_start(offsets[:], offs)
+            else:
+                load_projection(nc.sync, t)
             nc.sync.dma_start(windows[t][:], base[t * P : (t + 1) * P, :])
 
         weighted = [held.tile([P, N], BF16, name=f"weighted{k}") for k in range(D_BLOCKS)]

import concourse.mybir as mybir

F32, BF16, U16 = mybir.dt.float32, mybir.dt.bfloat16, mybir.dt.uint16
MULT, ADD = mybir.AluOpType.mult, mybir.AluOpType.add

P = 128
D = 256
N = 256
C = 384
S = 1024
D_BLOCKS = D // P
C_BLOCKS = C // P

FLOPS = 2 * D * C * N


def tile_typeenhancedgcndeepseek0_kernel(tc, base, h, pw, w, b, offs, out):
    nc = tc.nc
    with (
        tc.tile_pool(name="held", bufs=1) as held,
        tc.psum_pool(name="psum", bufs=1) as psum,
    ):
        tokens = [held.tile([P, N], F32, name=f"tokens{k}") for k in range(D_BLOCKS)]
        weight_of_token = held.tile([P, N], F32, name="weight_of_token")
        offsets = held.tile([P, N // 16], U16, name="offsets")
        projection = [held.tile([P, D_BLOCKS, P], BF16, name=f"projection{t}") for t in range(C_BLOCKS)]
        bias_column = [held.tile([P, 1], F32, name=f"bias_column{t}") for t in range(C_BLOCKS)]
        windows = [held.tile([P, S], F32, name=f"window{t}") for t in range(C_BLOCKS)]

        def load_projection(queue, t):
            queue.dma_start(
                projection[t][:], w[:, t * P : (t + 1) * P].rearrange("(k d) c -> d k c", d=P)
            )

        nc.scalar.dma_start(weight_of_token[:], pw.to_broadcast([P, N]))
        load_projection(nc.scalar, 0)

        for k in range(D_BLOCKS):
            nc.sync.dma_start(tokens[k][:], h[k * P : (k + 1) * P, :])
        for t in range(C_BLOCKS):
            nc.sync.dma_start(bias_column[t][:], b[t * P : (t + 1) * P, :])
            if t == 0:
                nc.sync.dma_start(offsets[:], offs)
            else:
                load_projection(nc.sync, t)
            nc.sync.dma_start(windows[t][:], base[t * P : (t + 1) * P, :])

        weighted = [held.tile([P, N], BF16, name=f"weighted{k}") for k in range(D_BLOCKS)]
        for k in range(D_BLOCKS):
            nc.vector.tensor_tensor(weighted[k][:], tokens[k][:], weight_of_token[:], MULT)

        for t in range(C_BLOCKS):
            product = psum.tile([P, N], F32, name="product")
            for k in range(D_BLOCKS):
                nc.tensor.matmul(
                    product[:],
                    projection[t][:, k, :],
                    weighted[k][:],
                    start=(k == 0),
                    stop=(k == D_BLOCKS - 1),
                )
            bias_of_token = held.tile([P, N], F32, name=f"bias_of_token{t}")
            projected = held.tile([P, N], F32, name=f"projected{t}")
            if t == 0:
                nc.vector.tensor_copy(bias_of_token[:], bias_column[t][:].to_broadcast([P, N]))
                nc.vector.tensor_copy(projected[:], product[:])
            else:
                nc.scalar.copy(bias_of_token[:], bias_column[t][:].to_broadcast([P, N]))
                nc.scalar.copy(projected[:], product[:])
            nc.vector.tensor_tensor(windows[t][:].indirect(offsets[:]), projected[:], bias_of_token[:], ADD)
            nc.sync.dma_start(out[t * P : (t + 1) * P, :], windows[t][:])
